import numpy as np
import ml_dtypes


def mxq(x, axis, fmt="e4m3"):
    dtype, down = {"e4m3": (ml_dtypes.float8_e4m3fn, 7), "e5m2": (ml_dtypes.float8_e5m2, 14)}[fmt]
    v = np.moveaxis(np.asarray(x, np.float32).astype(ml_dtypes.bfloat16).astype(np.float64), axis, -1)
    blocks = v.reshape(v.shape[:-1] + (-1, 32))
    amax = np.abs(blocks).max(-1, keepdims=True)
    byte = np.maximum(np.where(amax > 0, np.frexp(amax)[1] - 1 + 127, 0) - down, 1)
    scale = np.exp2(byte - 127.0)
    codes = (blocks / scale).astype(np.float32).astype(dtype).astype(np.float64)
    return np.moveaxis((codes * scale).reshape(v.shape), -1, axis)


WIDE = False


def mx_kscale(k):
    if not WIDE:
        return np.ones(k)
    levels = np.array([10, -10, 5, -5, 0])
    a = np.random.permutation(np.resize(levels, k // 512 * 4)).reshape(k // 512, 4)
    idx = np.arange(k)
    return np.exp2(a[idx // 512, idx % 128 // 32])


BF16 = ml_dtypes.bfloat16


def bf(x):
    return np.asarray(x, np.float32).astype(BF16)


def f64(x):
    return np.asarray(x).astype(np.float64)


B, S, D, E, EV, F, G = 4, 1024, 1024, 512, 256, 2048, 16
C = D // G
EPS_GN = 1e-5
EPS_L2 = 1e-12


def group_norm(x, gamma, beta):
    xg = x.reshape(B, S, G, C)
    mean = xg.mean(axis=(1, 3), keepdims=True)
    var = np.square(xg - mean).mean(axis=(1, 3), keepdims=True)
    xn = ((xg - mean) / np.sqrt(var + EPS_GN)).reshape(B, S, D)
    return xn * gamma + beta


def l2norm(u):
    n = np.sqrt(np.sum(u * u, axis=-1, keepdims=True))
    return u / np.maximum(n, EPS_L2)


def draw_stream():
    lev = np.repeat(np.random.standard_normal((B, 1, G)) * 0.5, C, axis=2)
    spr = np.repeat(np.random.uniform(0.5, 2.0, (B, 1, G)), C, axis=2)
    return np.random.standard_normal((B, S, D)) * spr + lev


def setup_inputs():
    s = mx_kscale(D)
    w = 1.0 / np.sqrt(D)
    return {"x": bf(draw_stream()),
            "gn1_g": bf((1.0 + 0.1 * np.random.standard_normal(D)) * s),
            "gn1_b": bf(0.3 * np.random.standard_normal(D) * s),
            "wq": bf(np.random.standard_normal((E, D)) * w / s[None, :]),
            "wk": bf(np.random.standard_normal((E, D)) * w / s[None, :]),
            "wv": bf(np.random.standard_normal((EV, D)) * w / s[None, :])}


def reference(x, gn1_g, gn1_b, wq, wk, wv):
    h = group_norm(f64(x), f64(gn1_g), f64(gn1_b))
    hq = mxq(h, 2, "e4m3")
    q = l2norm(hq @ mxq(f64(wq), 1, "e4m3").T)
    k = l2norm(hq @ mxq(f64(wk), 1, "e4m3").T)
    v = hq @ mxq(f64(wv), 1, "e4m3").T
    return q, k, v

@@ -1,0 +1,300 @@
+from contextlib import ExitStack
+
+import concourse.mybir as mybir
+from concourse.masks import make_identity
+
+F32 = mybir.dt.float32
+BF16 = mybir.dt.bfloat16
+U32 = mybir.dt.uint32
+U8 = mybir.dt.uint8
+FP8X4 = mybir.dt.float8_e4m3fn_x4
+ALU = mybir.AluOpType
+ACT = mybir.ActivationFunctionType
+AXIS = mybir.AxisListType
+
+BATCH, SEQ, CHANNELS = 4, 1024, 1024
+E_QK, E_V = 512, 256
+E_ALL = 2 * E_QK + E_V
+GROUPS = 16
+GROUP_CHANNELS = CHANNELS // GROUPS
+EPS_GN = 1e-5
+EPS_L2 = 1e-12
+
+P = 128
+PACK = 4
+K_PASS = P * PACK
+PASSES = CHANNELS // K_PASS
+BLOCKS = CHANNELS // P
+T = SEQ // P
+TILES = BATCH * T
+UNIT = 4
+UNIT_COLS = UNIT * P
+STEP_BLOCKS = 2
+STEPS_PER_PASS = PACK // STEP_BLOCKS
+NORM_STEPS = BLOCKS // STEP_BLOCKS
+HALF_GROUP_COUNT = T * GROUP_CHANNELS // 2
+W_ROW_TILES = E_ALL // P
+
+LAG_WEIGHTS = 4
+LAG_COEF = T
+COEF_STEPS = 4
+LAG_NORM = LAG_COEF + COEF_STEPS
+LAG_PROJECT = LAG_NORM + UNIT + 1
+LAG_FINISH = LAG_PROJECT + 1
+SLOTS = TILES + LAG_FINISH
+
+FLOPS = 2 * BATCH * SEQ * CHANNELS * E_ALL
+
+
+def tile_retnetblock_pa_t_kernel(tc, x, gn1_g, gn1_b, wq, wk, wv, out_0, out_1, out_2):
+    nc = tc.nc
+    with ExitStack() as pools:
+        pools.enter_context(tc.manual_schedule())
+        const = pools.enter_context(tc.tile_pool(name="const", bufs=1))
+        x_pool = pools.enter_context(tc.tile_pool(name="x", bufs=BATCH))
+        w_pool = pools.enter_context(tc.tile_pool(name="w", bufs=2))
+        stat = pools.enter_context(tc.tile_pool(name="stat", bufs=2))
+        plane_pool = pools.enter_context(tc.tile_pool(name="planes", bufs=2))
+        grouped_pool = pools.enter_context(tc.tile_pool(name="grouped", bufs=2))
+        code_pool = pools.enter_context(tc.tile_pool(name="codes", bufs=3))
+        norm_pool = pools.enter_context(tc.tile_pool(name="norm", bufs=4))
+        out_pool = pools.enter_context(tc.tile_pool(name="out", bufs=3))
+        turned_psum = pools.enter_context(tc.psum_pool(name="turned_psum", bufs=2))
+        acc_psum = pools.enter_context(tc.psum_pool(name="acc_psum", bufs=5))
+        v_psum = pools.enter_context(tc.psum_pool(name="v_psum", bufs=1))
+
+        ident = const.tile([P, P], BF16)
+        make_identity(nc, ident[:])
+        ones = const.tile([P, P], F32)
+        nc.vector.memset(ones[:], 1.0)
+        half_ones = const.tile([P, 2, P], F32)
+        nc.vector.memset(half_ones[:], 0.0)
+        for h in range(2):
+            nc.vector.memset(half_ones[:, h, h * (P // 2) : (h + 1) * (P // 2)], 1.0)
+        minus_half = const.tile([P, 2], F32)
+        nc.gpsimd.memset(minus_half[:], -0.5)
+        one_col = const.tile([P, 1], F32)
+        nc.vector.memset(one_col[:], 1.0)
+        sqrt_col = const.tile([P, 1], F32)
+        nc.scalar.sqrt(out=sqrt_col[:], in_=one_col[:])
+
+        w_codes = const.tile([P, PASSES, E_ALL], U32, align_bytes=64)
+        w_scales = const.tile([P, PASSES, E_ALL], U8, align_bytes=64)
+
+        x_sb = []
+        for b in range(BATCH):
+            x_b = x_pool.tile([P, T, CHANNELS], BF16)
+            x_sb.append(x_b)
+        nc.sync.dma_start(out=x_sb[0][:], in_=x[0].rearrange("(m t) d -> m t d", t=T))
+        gb_rows = const.tile([P, P], BF16)
+        nc.vector.memset(gb_rows[:], 0.0)
+        nc.sync.dma_start(out=gb_rows[0:BLOCKS, :], in_=gn1_g.rearrange("(c p) -> c p", p=P))
+        nc.sync.dma_start(out=gb_rows[BLOCKS : 2 * BLOCKS, :], in_=gn1_b.rearrange("(c p) -> c p", p=P))
+        w_row_tiles = []
+        for w in (wq, wk, wv):
+            n_tiles = w.shape[0] // P
+            w_rows = const.tile([P, n_tiles, CHANNELS], BF16, name="w_rows_%d" % len(w_row_tiles))
+            nc.sync.dma_start(out=w_rows[:], in_=w.rearrange("(r p) k -> p r k", p=P))
+            for r in range(n_tiles):
+                w_row_tiles.append((w_rows, r, len(w_row_tiles) * P))
+        for b in range(1, BATCH):
+            nc.sync.dma_start(out=x_sb[b][:], in_=x[b].rearrange("(m t) d -> m t d", t=T))
+
+        gb_t = turned_psum.tile([P, P], BF16, tag="turned")
+        nc.tensor.transpose(gb_t[:], gb_rows[:], ident[:])
+        gb = const.tile([P, 2 * BLOCKS], F32)
+        nc.vector.tensor_copy(out=gb[:], in_=gb_t[:, 0 : 2 * BLOCKS])
+
+        st_of, coef_of, planes_of, grouped_of, codes_of, acc_of, v_of, out_of = {}, {}, {}, {}, {}, {}, {}, {}
+
+        def statistics_step(b, step):
+            if step == 0:
+                st_of[b] = stat.tile([P, GROUPS, 6], F32, name="st", bufs=BATCH)
+            for g in range(step * GROUPS // T, (step + 1) * GROUPS // T):
+                cols = slice(g * GROUP_CHANNELS, (g + 1) * GROUP_CHANNELS)
+                nc.vector.bn_stats(out=st_of[b][:, g, :], in_=x_sb[b][:, :, cols])
+
+        def weights_step(w_rows, r, col0):
+            w_t = turned_psum.tile([P, BLOCKS, P], BF16, tag="turned")
+            for c in range(BLOCKS):
+                nc.tensor.transpose(w_t[:, c, :], w_rows[:, r, c * P : (c + 1) * P], ident[:])
+            w_grouped = w_pool.tile([P, PASSES, P, PACK], BF16, align_bytes=64)
+            nc.scalar.copy(out=w_grouped[:], in_=w_t[:].rearrange("p (g j) n -> p g n j", j=PACK))
+            for g in range(PASSES):
+                nc.vector.quantize_mx(
+                    out=w_codes[:, g, col0 : col0 + P].bitcast(FP8X4),
+                    scales=w_scales[:, g, col0 : col0 + P],
+                    in_=w_grouped[:, g, :, :].rearrange("p n j -> p (n j)"),
+                )
+
+        def coefficients_step(b, step):
+            halves = st_of[b][:].rearrange("p g (h s) -> p g h s", s=3)
+            means = halves[:, :, :, 1]
+            spreads = halves[:, :, :, 2]
+            if step == 0:
+                moments = stat.tile([P, 2, GROUPS], F32)
+                nc.vector.tensor_reduce(out=moments[:, 1, :], in_=means, axis=AXIS.X, op=ALU.add)
+                mean_sum = acc_psum.tile([P, GROUPS], F32, tag="acc")
+                nc.tensor.matmul(out=mean_sum[:], lhsT=ones[:], rhs=moments[:, 1, :], start=True, stop=True)
+                coef_of[b] = {"moments": moments, "mean_sum": mean_sum}
+            elif step == 1:
+                moments = coef_of[b]["moments"]
+                mean_all = stat.tile([P, GROUPS], F32)
+                nc.vector.tensor_scalar_mul(out=mean_all[:], in0=coef_of[b]["mean_sum"][:], scalar1=1.0 / (2 * P))
+                dev = stat.tile([P, GROUPS, 2], F32)
+                nc.vector.tensor_tensor(
+                    out=dev[:], in0=means, in1=mean_all[:].unsqueeze(2).to_broadcast([P, GROUPS, 2]), op=ALU.subtract
+                )
+                dev_sq = stat.tile([P, GROUPS, 2], F32)
+                nc.vector.tensor_tensor(out=dev_sq[:], in0=dev[:], in1=dev[:], op=ALU.mult)
+                spread_all = stat.tile([P, GROUPS, 2], F32)
+                nc.vector.scalar_tensor_tensor(
+                    out=spread_all[:], in0=dev_sq[:], scalar=float(HALF_GROUP_COUNT), in1=spreads,
+                    op0=ALU.mult, op1=ALU.add,
+                )
+                nc.vector.tensor_reduce(out=moments[:, 0, :], in_=spread_all[:], axis=AXIS.X, op=ALU.add)
+                by_half = moments[:].rearrange("p s (c h) -> p s c h", h=2)
+                sums = acc_psum.tile([P, 2, BLOCKS], F32, tag="acc")
+                for h in range(2):
+                    nc.tensor.matmul(
+                        out=sums[:], lhsT=half_ones[:, h, :], rhs=by_half[:, :, :, h], start=(h == 0), stop=(h == 1)
+                    )
+                coef_of[b]["sums"] = sums
+            elif step == 2:
+                var_eps = stat.tile([P, BLOCKS], F32)
+                nc.vector.tensor_scalar(
+                    out=var_eps[:], in0=coef_of[b]["sums"][:, 0, :], scalar1=1.0 / (SEQ * GROUP_CHANNELS),
+                    scalar2=EPS_GN, op0=ALU.mult, op1=ALU.add,
+                )
+                inv_var = stat.tile([P, BLOCKS], F32)
+                nc.vector.reciprocal(out=inv_var[:], in_=var_eps[:])
+                rstd = stat.tile([P, BLOCKS], F32)
+                nc.scalar.sqrt(out=rstd[:], in_=inv_var[:])
+                coef_of[b]["rstd"] = rstd
+            else:
+                gain = stat.tile([P, BLOCKS], F32)
+                nc.vector.tensor_tensor(out=gain[:], in0=gb[:, 0:BLOCKS], in1=coef_of[b]["rstd"][:], op=ALU.mult)
+                minus_mean_gain = stat.tile([P, BLOCKS], F32)
+                nc.vector.scalar_tensor_tensor(
+                    out=minus_mean_gain[:], in0=coef_of[b]["sums"][:, 1, :], scalar=-1.0 / (2 * P), in1=gain[:],
+                    op0=ALU.mult, op1=ALU.mult,
+                )
+                shift = stat.tile([P, BLOCKS], F32)
+                nc.vector.tensor_tensor(
+                    out=shift[:], in0=minus_mean_gain[:], in1=gb[:, BLOCKS : 2 * BLOCKS], op=ALU.add
+                )
+                coef_of[b]["gain"] = gain
+                coef_of[b]["shift"] = shift
+
+        def normalise_step(u, step):
+            b, t0 = u // (T // UNIT), (u % (T // UNIT)) * UNIT
+            if step % STEPS_PER_PASS == 0:
+                planes_of[u] = plane_pool.tile([P, PACK, UNIT_COLS], BF16, name="planes")
+            x_t = turned_psum.tile([P, STEP_BLOCKS, UNIT, P], BF16, tag="turned")
+            for i in range(STEP_BLOCKS):
+                c = step * STEP_BLOCKS + i
+                for t in range(UNIT):
+                    nc.tensor.transpose(x_t[:, i, t, :], x_sb[b][:, t0 + t, c * P : (c + 1) * P], ident[:])
+            for i in range(STEP_BLOCKS):
+                c = step * STEP_BLOCKS + i
+                nc.vector.tensor_scalar(
+                    out=planes_of[u][:, c % PACK, :], in0=x_t[:, i, :, :].rearrange("p t m -> p (t m)"),
+                    scalar1=coef_of[b]["gain"][:, c : c + 1], scalar2=coef_of[b]["shift"][:, c : c + 1],
+                    op0=ALU.mult, op1=ALU.add,
+                )
+            if step % STEPS_PER_PASS == STEPS_PER_PASS - 1:
+                grouped_of[u] = grouped_pool.tile([P, UNIT_COLS, PACK], BF16, name="grouped", align_bytes=64)
+                nc.vector.tensor_copy(
+                    out=grouped_of[u][:].rearrange("p (c i) j -> p c j i", i=4),
+                    in_=planes_of[u][:].rearrange("p j (c i) -> p c j i", i=4),
+                )
+
+        def quantise_step(u, step):
+            if step % STEPS_PER_PASS != STEPS_PER_PASS - 1:
+                return
+            g = step // STEPS_PER_PASS
+            if g == 0:
+                h_codes = code_pool.tile([P, PASSES, UNIT_COLS], U32, align_bytes=64)
+                h_scales = code_pool.tile([P, PASSES, UNIT_COLS], U8, align_bytes=64)
+                codes_of[u] = (h_codes, h_scales)
+            h_codes, h_scales = codes_of[u]
+            nc.vector.quantize_mx(
+                out=h_codes[:, g, :].bitcast(FP8X4),
+                scales=h_scales[:, g, :],
+                in_=grouped_of[u][:].rearrange("p c j -> p (c j)"),
+            )
+
+        def project(acc, tile, cols):
+            h_codes, h_scales = codes_of[tile // UNIT]
+            rows = slice((tile % UNIT) * P, (tile % UNIT + 1) * P)
+            for g in range(PASSES):
+                nc.tensor.matmul_mx(
+                    out=acc,
+                    lhsT=h_codes[:, g, rows].bitcast(FP8X4),
+                    lhsT_scale=h_scales[:, g, rows],
+                    rhs=w_codes[:, g, cols].bitcast(FP8X4),
+                    rhs_scale=w_scales[:, g, cols],
+                    start=(g == 0),
+                    stop=(g == PASSES - 1),
+                )
+
+        def project_step(tile):
+            q_acc = acc_psum.tile([P, E_QK], F32, tag="acc")
+            k_acc = acc_psum.tile([P, E_QK], F32, tag="acc")
+            if tile % 2 == 0:
+                v_of[tile // 2] = v_psum.tile([P, 2, E_V], F32, name="v_acc")
+            project(q_acc[:], tile, slice(0, E_QK))
+            project(k_acc[:], tile, slice(E_QK, 2 * E_QK))
+            project(v_of[tile // 2][:, tile % 2, :], tile, slice(2 * E_QK, E_ALL))
+            sum_sq = norm_pool.tile([P, 2], F32)
+            for col, acc in enumerate((q_acc, k_acc)):
+                squares = norm_pool.tile([P, E_QK], BF16)
+                nc.scalar.activation(out=squares[:], in_=acc[:], func=ACT.Square, accum_out=sum_sq[:, col : col + 1])
+            floored = norm_pool.tile([P, 2], F32)
+            nc.gpsimd.tensor_scalar_max(out=floored[:], in0=sum_sq[:], scalar1=EPS_L2 * EPS_L2)
+            inv_norm = norm_pool.tile([P, 2], F32)
+            nc.gpsimd.tensor_tensor(out=inv_norm[:], in0=floored[:], in1=minus_half[:], op=ALU.pow)
+            acc_of[tile] = (q_acc, k_acc, inv_norm)
+
+        def store(dram, tile, tile_out):
+            b, t0 = tile // T, (tile % T) - (UNIT - 1)
+            nc.sync.dma_start(out=dram[b].rearrange("(m t) e -> m t e", t=T)[:, t0 : t0 + UNIT, :], in_=tile_out[:])
+
+        def copy_v_step(tile):
+            if tile % 2 == 1:
+                v_out = out_of[tile // UNIT][2]
+                nc.vector.tensor_copy(out=v_out[:, tile % UNIT - 1 : tile % UNIT + 1, :], in_=v_of[tile // 2][:])
+                if tile % UNIT == UNIT - 1:
+                    store(out_2, tile, v_out)
+
+        def finish_step(tile):
+            if tile % UNIT == 0:
+                q_out = out_pool.tile([P, UNIT, E_QK], F32)
+                k_out = out_pool.tile([P, UNIT, E_QK], F32)
+                v_out = out_pool.tile([P, UNIT, E_V], F32)
+                out_of[tile // UNIT] = (q_out, k_out, v_out)
+            q_out, k_out, v_out = out_of[tile // UNIT]
+            q_acc, k_acc, inv_norm = acc_of[tile]
+            nc.scalar.activation(out=q_out[:, tile % UNIT, :], in_=q_acc[:], func=ACT.Copy, scale=inv_norm[:, 0:1])
+            nc.scalar.activation(out=k_out[:, tile % UNIT, :], in_=k_acc[:], func=ACT.Copy, scale=inv_norm[:, 1:2])
+            if tile % UNIT == UNIT - 1:
+                store(out_0, tile, q_out)
+                store(out_1, tile, k_out)
+
+        for n in range(SLOTS):
+            if n >= LAG_FINISH:
+                copy_v_step(n - LAG_FINISH)
+            if 0 <= n - LAG_NORM < TILES:
+                normalise_step((n - LAG_NORM) // NORM_STEPS, (n - LAG_NORM) % NORM_STEPS)
+            if 0 <= n - LAG_COEF < TILES and (n - LAG_COEF) % T < COEF_STEPS:
+                coefficients_step((n - LAG_COEF) // T, (n - LAG_COEF) % T)
+            if n < TILES:
+                statistics_step(n // T, n % T)
+            if 0 <= n - LAG_WEIGHTS < W_ROW_TILES:
+                weights_step(*w_row_tiles[n - LAG_WEIGHTS])
+            if 0 <= n - LAG_NORM < TILES:
+                quantise_step((n - LAG_NORM) // NORM_STEPS, (n - LAG_NORM) % NORM_STEPS)
+            if 0 <= n - LAG_PROJECT < TILES:
+                project_step(n - LAG_PROJECT)
+            if n >= LAG_FINISH:
+                finish_step(n - LAG_FINISH)

@@ -37,8 +37,8 @@ W_ROW_TILES = E_ALL // P
 
 LAG_WEIGHTS = 4
 LAG_COEF = T
-COEF_STEPS = 4
-LAG_NORM = LAG_COEF + COEF_STEPS
+COEF_STEPS = 5
+LAG_NORM = LAG_COEF + COEF_STEPS + 1
 LAG_PROJECT = LAG_NORM + UNIT + 1
 LAG_FINISH = LAG_PROJECT + 1
 SLOTS = TILES + LAG_FINISH
@@ -71,12 +71,8 @@ def tile_retnetblock_pa_t_kernel(tc, x, gn1_g, gn1_b, wq, wk, wv, out_0, out_1, 
         nc.vector.memset(half_ones[:], 0.0)
         for h in range(2):
             nc.vector.memset(half_ones[:, h, h * (P // 2) : (h + 1) * (P // 2)], 1.0)
-        minus_half = const.tile([P, 2], F32)
+        minus_half = const.tile([P, BLOCKS], F32)
         nc.gpsimd.memset(minus_half[:], -0.5)
-        one_col = const.tile([P, 1], F32)
-        nc.vector.memset(one_col[:], 1.0)
-        sqrt_col = const.tile([P, 1], F32)
-        nc.scalar.sqrt(out=sqrt_col[:], in_=one_col[:])
 
         w_codes = const.tile([P, PASSES, E_ALL], U32, align_bytes=64)
         w_scales = const.tile([P, PASSES, E_ALL], U8, align_bytes=64)
@@ -133,56 +129,56 @@ def tile_retnetblock_pa_t_kernel(tc, x, gn1_g, gn1_b, wq, wk, wv, out_0, out_1, 
             spreads = halves[:, :, :, 2]
             if step == 0:
                 moments = stat.tile([P, 2, GROUPS], F32)
-                nc.vector.tensor_reduce(out=moments[:, 1, :], in_=means, axis=AXIS.X, op=ALU.add)
-                mean_sum = acc_psum.tile([P, GROUPS], F32, tag="acc")
-                nc.tensor.matmul(out=mean_sum[:], lhsT=ones[:], rhs=moments[:, 1, :], start=True, stop=True)
-                coef_of[b] = {"moments": moments, "mean_sum": mean_sum}
+                nc.gpsimd.tensor_tensor(out=moments[:, 1, :], in0=means[:, :, 0], in1=means[:, :, 1], op=ALU.add)
+                spread_sum = stat.tile([P, GROUPS], F32)
+                nc.gpsimd.tensor_tensor(out=spread_sum[:], in0=spreads[:, :, 0], in1=spreads[:, :, 1], op=ALU.add)
+                spread_part = stat.tile([P, GROUPS], F32)
+                nc.gpsimd.tensor_scalar(
+                    out=spread_part[:], in0=spread_sum[:], scalar1=1.0 / HALF_GROUP_COUNT, scalar2=0.0,
+                    op0=ALU.mult, op1=ALU.add,
+                )
+                coef_of[b] = {"moments": moments, "spread_part": spread_part}
             elif step == 1:
+                mean_sum = acc_psum.tile([P, GROUPS], F32, tag="acc")
+                nc.tensor.matmul(out=mean_sum[:], lhsT=ones[:], rhs=coef_of[b]["moments"][:, 1, :], start=True, stop=True)
+                coef_of[b]["mean_sum"] = mean_sum
+            elif step == 2:
                 moments = coef_of[b]["moments"]
                 mean_all = stat.tile([P, GROUPS], F32)
-                nc.vector.tensor_scalar_mul(out=mean_all[:], in0=coef_of[b]["mean_sum"][:], scalar1=1.0 / (2 * P))
+                nc.scalar.activation(out=mean_all[:], in_=coef_of[b]["mean_sum"][:], func=ACT.Copy, scale=1.0 / (2 * P))
                 dev = stat.tile([P, GROUPS, 2], F32)
-                nc.vector.tensor_tensor(
+                nc.gpsimd.tensor_tensor(
                     out=dev[:], in0=means, in1=mean_all[:].unsqueeze(2).to_broadcast([P, GROUPS, 2]), op=ALU.subtract
                 )
                 dev_sq = stat.tile([P, GROUPS, 2], F32)
-                nc.vector.tensor_tensor(out=dev_sq[:], in0=dev[:], in1=dev[:], op=ALU.mult)
-                spread_all = stat.tile([P, GROUPS, 2], F32)
-                nc.vector.scalar_tensor_tensor(
-                    out=spread_all[:], in0=dev_sq[:], scalar=float(HALF_GROUP_COUNT), in1=spreads,
-                    op0=ALU.mult, op1=ALU.add,
+                nc.gpsimd.tensor_tensor(out=dev_sq[:], in0=dev[:], in1=dev[:], op=ALU.mult)
+                dev_sq_sum = stat.tile([P, GROUPS], F32)
+                nc.gpsimd.tensor_tensor(out=dev_sq_sum[:], in0=dev_sq[:, :, 0], in1=dev_sq[:, :, 1], op=ALU.add)
+                nc.gpsimd.tensor_tensor(
+                    out=moments[:, 0, :], in0=dev_sq_sum[:], in1=coef_of[b]["spread_part"][:], op=ALU.add
                 )
-                nc.vector.tensor_reduce(out=moments[:, 0, :], in_=spread_all[:], axis=AXIS.X, op=ALU.add)
-                by_half = moments[:].rearrange("p s (c h) -> p s c h", h=2)
+            elif step == 3:
+                by_half = coef_of[b]["moments"][:].rearrange("p s (c h) -> p s c h", h=2)
                 sums = acc_psum.tile([P, 2, BLOCKS], F32, tag="acc")
                 for h in range(2):
                     nc.tensor.matmul(
                         out=sums[:], lhsT=half_ones[:, h, :], rhs=by_half[:, :, :, h], start=(h == 0), stop=(h == 1)
                     )
                 coef_of[b]["sums"] = sums
-            elif step == 2:
-                var_eps = stat.tile([P, BLOCKS], F32)
-                nc.vector.tensor_scalar(
-                    out=var_eps[:], in0=coef_of[b]["sums"][:, 0, :], scalar1=1.0 / (SEQ * GROUP_CHANNELS),
-                    scalar2=EPS_GN, op0=ALU.mult, op1=ALU.add,
-                )
-                inv_var = stat.tile([P, BLOCKS], F32)
-                nc.vector.reciprocal(out=inv_var[:], in_=var_eps[:])
-                rstd = stat.tile([P, BLOCKS], F32)
-                nc.scalar.sqrt(out=rstd[:], in_=inv_var[:])
-                coef_of[b]["rstd"] = rstd
             else:
+                sums = coef_of[b]["sums"]
+                var_eps = stat.tile([P, BLOCKS], F32)
+                nc.scalar.activation(out=var_eps[:], in_=sums[:, 0, :], func=ACT.Copy, scale=1.0 / (2 * P), bias=EPS_GN)
+                mean = stat.tile([P, BLOCKS], F32)
+                nc.scalar.activation(out=mean[:], in_=sums[:, 1, :], func=ACT.Copy, scale=1.0 / (2 * P))
+                rstd = stat.tile([P, BLOCKS], F32)
+                nc.gpsimd.tensor_tensor(out=rstd[:], in0=var_eps[:], in1=minus_half[:], op=ALU.pow)
                 gain = stat.tile([P, BLOCKS], F32)
-                nc.vector.tensor_tensor(out=gain[:], in0=gb[:, 0:BLOCKS], in1=coef_of[b]["rstd"][:], op=ALU.mult)
-                minus_mean_gain = stat.tile([P, BLOCKS], F32)
-                nc.vector.scalar_tensor_tensor(
-                    out=minus_mean_gain[:], in0=coef_of[b]["sums"][:, 1, :], scalar=-1.0 / (2 * P), in1=gain[:],
-                    op0=ALU.mult, op1=ALU.mult,
-                )
+                nc.gpsimd.tensor_tensor(out=gain[:], in0=gb[:, 0:BLOCKS], in1=rstd[:], op=ALU.mult)
+                mean_gain = stat.tile([P, BLOCKS], F32)
+                nc.gpsimd.tensor_tensor(out=mean_gain[:], in0=mean[:], in1=gain[:], op=ALU.mult)
                 shift = stat.tile([P, BLOCKS], F32)
-                nc.vector.tensor_tensor(
-                    out=shift[:], in0=minus_mean_gain[:], in1=gb[:, BLOCKS : 2 * BLOCKS], op=ALU.add
-                )
+                nc.gpsimd.tensor_tensor(out=shift[:], in0=gb[:, BLOCKS : 2 * BLOCKS], in1=mean_gain[:], op=ALU.subtract)
                 coef_of[b]["gain"] = gain
                 coef_of[b]["shift"] = shift
 
@@ -253,7 +249,7 @@ def tile_retnetblock_pa_t_kernel(tc, x, gn1_g, gn1_b, wq, wk, wv, out_0, out_1, 
             floored = norm_pool.tile([P, 2], F32)
             nc.gpsimd.tensor_scalar_max(out=floored[:], in0=sum_sq[:], scalar1=EPS_L2 * EPS_L2)
             inv_norm = norm_pool.tile([P, 2], F32)
-            nc.gpsimd.tensor_tensor(out=inv_norm[:], in0=floored[:], in1=minus_half[:], op=ALU.pow)
+            nc.gpsimd.tensor_tensor(out=inv_norm[:], in0=floored[:], in1=minus_half[:, 0:2], op=ALU.pow)
             acc_of[tile] = (q_acc, k_acc, inv_norm)
 
         def store(dram, tile, tile_out):

@@ -39,7 +39,7 @@ LAG_WEIGHTS = 4
 LAG_COEF = T
 COEF_STEPS = 5
 LAG_NORM = LAG_COEF + COEF_STEPS + 1
-LAG_PROJECT = LAG_NORM + UNIT + 1
+LAG_PROJECT = LAG_NORM + UNIT
 LAG_FINISH = LAG_PROJECT + 1
 SLOTS = TILES + LAG_FINISH
 
@@ -58,7 +58,7 @@ def tile_retnetblock_pa_t_kernel(tc, x, gn1_g, gn1_b, wq, wk, wv, out_0, out_1, 
         grouped_pool = pools.enter_context(tc.tile_pool(name="grouped", bufs=2))
         code_pool = pools.enter_context(tc.tile_pool(name="codes", bufs=3))
         norm_pool = pools.enter_context(tc.tile_pool(name="norm", bufs=4))
-        out_pool = pools.enter_context(tc.tile_pool(name="out", bufs=3))
+        out_pool = pools.enter_context(tc.tile_pool(name="out", bufs=4))
         turned_psum = pools.enter_context(tc.psum_pool(name="turned_psum", bufs=2))
         acc_psum = pools.enter_context(tc.psum_pool(name="acc_psum", bufs=5))
         v_psum = pools.enter_context(tc.psum_pool(name="v_psum", bufs=1))
@@ -182,7 +182,7 @@ def tile_retnetblock_pa_t_kernel(tc, x, gn1_g, gn1_b, wq, wk, wv, out_0, out_1, 
                 coef_of[b]["gain"] = gain
                 coef_of[b]["shift"] = shift
 
-        def normalise_step(u, step):
+        def normalise_step(u, step, by_scalar):
             b, t0 = u // (T // UNIT), (u % (T // UNIT)) * UNIT
             if step % STEPS_PER_PASS == 0:
                 planes_of[u] = plane_pool.tile([P, PACK, UNIT_COLS], BF16, name="planes")
@@ -193,11 +193,16 @@ def tile_retnetblock_pa_t_kernel(tc, x, gn1_g, gn1_b, wq, wk, wv, out_0, out_1, 
                     nc.tensor.transpose(x_t[:, i, t, :], x_sb[b][:, t0 + t, c * P : (c + 1) * P], ident[:])
             for i in range(STEP_BLOCKS):
                 c = step * STEP_BLOCKS + i
-                nc.vector.tensor_scalar(
-                    out=planes_of[u][:, c % PACK, :], in0=x_t[:, i, :, :].rearrange("p t m -> p (t m)"),
-                    scalar1=coef_of[b]["gain"][:, c : c + 1], scalar2=coef_of[b]["shift"][:, c : c + 1],
-                    op0=ALU.mult, op1=ALU.add,
-                )
+                h_plane = planes_of[u][:, c % PACK, :]
+                x_plane = x_t[:, i, :, :].rearrange("p t m -> p (t m)")
+                gain = coef_of[b]["gain"][:, c : c + 1]
+                shift = coef_of[b]["shift"][:, c : c + 1]
+                if by_scalar:
+                    nc.scalar.activation(out=h_plane, in_=x_plane, func=ACT.Identity, scale=gain, bias=shift)
+                else:
+                    nc.vector.tensor_scalar(
+                        out=h_plane, in0=x_plane, scalar1=gain, scalar2=shift, op0=ALU.mult, op1=ALU.add
+                    )
             if step % STEPS_PER_PASS == STEPS_PER_PASS - 1:
                 grouped_of[u] = grouped_pool.tile([P, UNIT_COLS, PACK], BF16, name="grouped", align_bytes=64)
                 nc.vector.tensor_copy(
@@ -253,27 +258,29 @@ def tile_retnetblock_pa_t_kernel(tc, x, gn1_g, gn1_b, wq, wk, wv, out_0, out_1, 
             acc_of[tile] = (q_acc, k_acc, inv_norm)
 
         def store(dram, tile, tile_out):
-            b, t0 = tile // T, (tile % T) - (UNIT - 1)
-            nc.sync.dma_start(out=dram[b].rearrange("(m t) e -> m t e", t=T)[:, t0 : t0 + UNIT, :], in_=tile_out[:])
+            b, t = tile // T, tile % T
+            nc.sync.dma_start(out=dram[b].rearrange("(m t) e -> m t e", t=T)[:, t - 1 : t + 1, :], in_=tile_out[:])
 
         def copy_v_step(tile):
             if tile % 2 == 1:
-                v_out = out_of[tile // UNIT][2]
-                nc.vector.tensor_copy(out=v_out[:, tile % UNIT - 1 : tile % UNIT + 1, :], in_=v_of[tile // 2][:])
-                if tile % UNIT == UNIT - 1:
-                    store(out_2, tile, v_out)
+                v_out = out_of[tile // 2][2]
+                nc.scalar.copy(out=v_out[:], in_=v_of[tile // 2][:])
+                store(out_2, tile, v_out)
 
-        def finish_step(tile):
-            if tile % UNIT == 0:
-                q_out = out_pool.tile([P, UNIT, E_QK], F32)
-                k_out = out_pool.tile([P, UNIT, E_QK], F32)
-                v_out = out_pool.tile([P, UNIT, E_V], F32)
-                out_of[tile // UNIT] = (q_out, k_out, v_out)
-            q_out, k_out, v_out = out_of[tile // UNIT]
+        def finish_step(tile, k_by_vector):
+            if tile % 2 == 0:
+                q_out = out_pool.tile([P, 2, E_QK], F32)
+                k_out = out_pool.tile([P, 2, E_QK], F32)
+                v_out = out_pool.tile([P, 2, E_V], F32)
+                out_of[tile // 2] = (q_out, k_out, v_out)
+            q_out, k_out, v_out = out_of[tile // 2]
             q_acc, k_acc, inv_norm = acc_of[tile]
-            nc.scalar.activation(out=q_out[:, tile % UNIT, :], in_=q_acc[:], func=ACT.Copy, scale=inv_norm[:, 0:1])
-            nc.scalar.activation(out=k_out[:, tile % UNIT, :], in_=k_acc[:], func=ACT.Copy, scale=inv_norm[:, 1:2])
-            if tile % UNIT == UNIT - 1:
+            nc.scalar.activation(out=q_out[:, tile % 2, :], in_=q_acc[:], func=ACT.Copy, scale=inv_norm[:, 0:1])
+            if k_by_vector:
+                nc.vector.tensor_scalar_mul(out=k_out[:, tile % 2, :], in0=k_acc[:], scalar1=inv_norm[:, 1:2])
+            else:
+                nc.scalar.activation(out=k_out[:, tile % 2, :], in_=k_acc[:], func=ACT.Copy, scale=inv_norm[:, 1:2])
+            if tile % 2 == 1:
                 store(out_0, tile, q_out)
                 store(out_1, tile, k_out)
 
@@ -281,7 +288,7 @@ def tile_retnetblock_pa_t_kernel(tc, x, gn1_g, gn1_b, wq, wk, wv, out_0, out_1, 
             if n >= LAG_FINISH:
                 copy_v_step(n - LAG_FINISH)
             if 0 <= n - LAG_NORM < TILES:
-                normalise_step((n - LAG_NORM) // NORM_STEPS, (n - LAG_NORM) % NORM_STEPS)
+                normalise_step((n - LAG_NORM) // NORM_STEPS, (n - LAG_NORM) % NORM_STEPS, n < LAG_PROJECT)
             if 0 <= n - LAG_COEF < TILES and (n - LAG_COEF) % T < COEF_STEPS:
                 coefficients_step((n - LAG_COEF) // T, (n - LAG_COEF) % T)
             if n < TILES:
@@ -293,4 +300,4 @@ def tile_retnetblock_pa_t_kernel(tc, x, gn1_g, gn1_b, wq, wk, wv, out_0, out_1, 
             if 0 <= n - LAG_PROJECT < TILES:
                 project_step(n - LAG_PROJECT)
             if n >= LAG_FINISH:
-                finish_step(n - LAG_FINISH)
+                finish_step(n - LAG_FINISH, n >= LAG_NORM + TILES)

@@ -29,13 +29,11 @@ T = SEQ // P
 TILES = BATCH * T
 UNIT = 4
 UNIT_COLS = UNIT * P
-STEP_BLOCKS = 2
-STEPS_PER_PASS = PACK // STEP_BLOCKS
-NORM_STEPS = BLOCKS // STEP_BLOCKS
+NORM_STEPS = 2 * PASSES
 HALF_GROUP_COUNT = T * GROUP_CHANNELS // 2
 W_ROW_TILES = E_ALL // P
 
-LAG_WEIGHTS = 4
+LAG_WEIGHTS = 5
 LAG_COEF = T
 COEF_STEPS = 5
 LAG_NORM = LAG_COEF + COEF_STEPS + 1
@@ -52,7 +50,7 @@ def tile_retnetblock_pa_t_kernel(tc, x, gn1_g, gn1_b, wq, wk, wv, out_0, out_1, 
         pools.enter_context(tc.manual_schedule())
         const = pools.enter_context(tc.tile_pool(name="const", bufs=1))
         x_pool = pools.enter_context(tc.tile_pool(name="x", bufs=BATCH))
-        w_pool = pools.enter_context(tc.tile_pool(name="w", bufs=2))
+        w_pool = pools.enter_context(tc.tile_pool(name="w", bufs=3))
         stat = pools.enter_context(tc.tile_pool(name="stat", bufs=2))
         plane_pool = pools.enter_context(tc.tile_pool(name="planes", bufs=2))
         grouped_pool = pools.enter_context(tc.tile_pool(name="grouped", bufs=2))
@@ -81,7 +79,12 @@ def tile_retnetblock_pa_t_kernel(tc, x, gn1_g, gn1_b, wq, wk, wv, out_0, out_1, 
         for b in range(BATCH):
             x_b = x_pool.tile([P, T, CHANNELS], BF16)
             x_sb.append(x_b)
-        nc.sync.dma_start(out=x_sb[0][:], in_=x[0].rearrange("(m t) d -> m t d", t=T))
+
+        def load_x(b):
+            for cols in (slice(0, CHANNELS // 2), slice(CHANNELS // 2, CHANNELS)):
+                nc.sync.dma_start(out=x_sb[b][:, :, cols], in_=x[b].rearrange("(m t) d -> m t d", t=T)[:, :, cols])
+
+        load_x(0)
         gb_rows = const.tile([P, P], BF16)
         nc.vector.memset(gb_rows[:], 0.0)
         nc.sync.dma_start(out=gb_rows[0:BLOCKS, :], in_=gn1_g.rearrange("(c p) -> c p", p=P))
@@ -91,17 +94,18 @@ def tile_retnetblock_pa_t_kernel(tc, x, gn1_g, gn1_b, wq, wk, wv, out_0, out_1, 
             n_tiles = w.shape[0] // P
             w_rows = const.tile([P, n_tiles, CHANNELS], BF16, name="w_rows_%d" % len(w_row_tiles))
             nc.sync.dma_start(out=w_rows[:], in_=w.rearrange("(r p) k -> p r k", p=P))
+            col0 = len(w_row_tiles) * P
             for r in range(n_tiles):
-                w_row_tiles.append((w_rows, r, len(w_row_tiles) * P))
+                w_row_tiles.append((w_rows, r, n_tiles, col0))
         for b in range(1, BATCH):
-            nc.sync.dma_start(out=x_sb[b][:], in_=x[b].rearrange("(m t) d -> m t d", t=T))
+            load_x(b)
 
         gb_t = turned_psum.tile([P, P], BF16, tag="turned")
         nc.tensor.transpose(gb_t[:], gb_rows[:], ident[:])
         gb = const.tile([P, 2 * BLOCKS], F32)
-        nc.vector.tensor_copy(out=gb[:], in_=gb_t[:, 0 : 2 * BLOCKS])
+        nc.scalar.copy(out=gb[:], in_=gb_t[:, 0 : 2 * BLOCKS])
 
-        st_of, coef_of, planes_of, grouped_of, codes_of, acc_of, v_of, out_of = {}, {}, {}, {}, {}, {}, {}, {}
+        st_of, coef_of, planes_of, grouped_of, codes_of, acc_of, v_of, out_of, w_grouped_of = {}, {}, {}, {}, {}, {}, {}, {}, {}
 
         def statistics_step(b, step):
             if step == 0:
@@ -110,18 +114,24 @@ def tile_retnetblock_pa_t_kernel(tc, x, gn1_g, gn1_b, wq, wk, wv, out_0, out_1, 
                 cols = slice(g * GROUP_CHANNELS, (g + 1) * GROUP_CHANNELS)
                 nc.vector.bn_stats(out=st_of[b][:, g, :], in_=x_sb[b][:, :, cols])
 
-        def weights_step(w_rows, r, col0):
+        def weights_step(w_rows, r, n_tiles, col0):
             w_t = turned_psum.tile([P, BLOCKS, P], BF16, tag="turned")
             for c in range(BLOCKS):
                 nc.tensor.transpose(w_t[:, c, :], w_rows[:, r, c * P : (c + 1) * P], ident[:])
-            w_grouped = w_pool.tile([P, PASSES, P, PACK], BF16, align_bytes=64)
-            nc.scalar.copy(out=w_grouped[:], in_=w_t[:].rearrange("p (g j) n -> p g n j", j=PACK))
-            for g in range(PASSES):
-                nc.vector.quantize_mx(
-                    out=w_codes[:, g, col0 : col0 + P].bitcast(FP8X4),
-                    scales=w_scales[:, g, col0 : col0 + P],
-                    in_=w_grouped[:, g, :, :].rearrange("p n j -> p (n j)"),
-                )
+            if r == 0:
+                w_grouped_of[col0] = w_pool.tile([P, PASSES, n_tiles * P, PACK], BF16, name="w_grouped", align_bytes=64)
+            w_grouped = w_grouped_of[col0]
+            nc.scalar.copy(
+                out=w_grouped[:, :, r * P : (r + 1) * P, :], in_=w_t[:].rearrange("p (g j) n -> p g n j", j=PACK)
+            )
+            if r == n_tiles - 1:
+                cols = slice(col0, col0 + n_tiles * P)
+                for g in range(PASSES):
+                    nc.vector.quantize_mx(
+                        out=w_codes[:, g, cols].bitcast(FP8X4),
+                        scales=w_scales[:, g, cols],
+                        in_=w_grouped[:, g, :, :].rearrange("p n j -> p (n j)"),
+                    )
 
         def coefficients_step(b, step):
             halves = st_of[b][:].rearrange("p g (h s) -> p g h s", s=3)
@@ -184,26 +194,32 @@ def tile_retnetblock_pa_t_kernel(tc, x, gn1_g, gn1_b, wq, wk, wv, out_0, out_1, 
 
         def normalise_step(u, step, by_scalar):
             b, t0 = u // (T // UNIT), (u % (T // UNIT)) * UNIT
-            if step % STEPS_PER_PASS == 0:
+            g = step // 2
+            if step % 2 == 0:
+                banks = []
+                for half in range(2):
+                    x_t = turned_psum.tile([P, PACK // 2, UNIT, P], BF16, tag="turned")
+                    banks.append(x_t)
+                for j in range(PACK):
+                    c = g * PACK + j
+                    for t in range(UNIT):
+                        nc.tensor.transpose(
+                            banks[j // 2][:, j % 2, t, :], x_sb[b][:, t0 + t, c * P : (c + 1) * P], ident[:]
+                        )
                 planes_of[u] = plane_pool.tile([P, PACK, UNIT_COLS], BF16, name="planes")
-            x_t = turned_psum.tile([P, STEP_BLOCKS, UNIT, P], BF16, tag="turned")
-            for i in range(STEP_BLOCKS):
-                c = step * STEP_BLOCKS + i
-                for t in range(UNIT):
-                    nc.tensor.transpose(x_t[:, i, t, :], x_sb[b][:, t0 + t, c * P : (c + 1) * P], ident[:])
-            for i in range(STEP_BLOCKS):
-                c = step * STEP_BLOCKS + i
-                h_plane = planes_of[u][:, c % PACK, :]
-                x_plane = x_t[:, i, :, :].rearrange("p t m -> p (t m)")
-                gain = coef_of[b]["gain"][:, c : c + 1]
-                shift = coef_of[b]["shift"][:, c : c + 1]
-                if by_scalar:
-                    nc.scalar.activation(out=h_plane, in_=x_plane, func=ACT.Identity, scale=gain, bias=shift)
-                else:
-                    nc.vector.tensor_scalar(
-                        out=h_plane, in0=x_plane, scalar1=gain, scalar2=shift, op0=ALU.mult, op1=ALU.add
-                    )
-            if step % STEPS_PER_PASS == STEPS_PER_PASS - 1:
+                for j in range(PACK):
+                    c = g * PACK + j
+                    h_plane = planes_of[u][:, j, :]
+                    x_plane = banks[j // 2][:, j % 2, :, :].rearrange("p t m -> p (t m)")
+                    gain = coef_of[b]["gain"][:, c : c + 1]
+                    shift = coef_of[b]["shift"][:, c : c + 1]
+                    if by_scalar:
+                        nc.scalar.activation(out=h_plane, in_=x_plane, func=ACT.Identity, scale=gain, bias=shift)
+                    else:
+                        nc.vector.tensor_scalar(
+                            out=h_plane, in0=x_plane, scalar1=gain, scalar2=shift, op0=ALU.mult, op1=ALU.add
+                        )
+            else:
                 grouped_of[u] = grouped_pool.tile([P, UNIT_COLS, PACK], BF16, name="grouped", align_bytes=64)
                 nc.vector.tensor_copy(
                     out=grouped_of[u][:].rearrange("p (c i) j -> p c j i", i=4),
@@ -211,9 +227,9 @@ def tile_retnetblock_pa_t_kernel(tc, x, gn1_g, gn1_b, wq, wk, wv, out_0, out_1, 
                 )
 
         def quantise_step(u, step):
-            if step % STEPS_PER_PASS != STEPS_PER_PASS - 1:
+            if step % 2 == 0:
                 return
-            g = step // STEPS_PER_PASS
+            g = step // 2
             if g == 0:
                 h_codes = code_pool.tile([P, PASSES, UNIT_COLS], U32, align_bytes=64)
                 h_scales = code_pool.tile([P, PASSES, UNIT_COLS], U8, align_bytes=64)
@@ -300,4 +316,4 @@ def tile_retnetblock_pa_t_kernel(tc, x, gn1_g, gn1_b, wq, wk, wv, out_0, out_1, 
             if 0 <= n - LAG_PROJECT < TILES:
                 project_step(n - LAG_PROJECT)
             if n >= LAG_FINISH:
-                finish_step(n - LAG_FINISH, n >= LAG_NORM + TILES)
+                finish_step(n - LAG_FINISH, n >= TILES)

from contextlib import ExitStack

import concourse.mybir as mybir
from concourse.masks import make_identity

F32 = mybir.dt.float32
BF16 = mybir.dt.bfloat16
U32 = mybir.dt.uint32
U8 = mybir.dt.uint8
FP8X4 = mybir.dt.float8_e4m3fn_x4
ALU = mybir.AluOpType
ACT = mybir.ActivationFunctionType
AXIS = mybir.AxisListType

BATCH, SEQ, CHANNELS = 4, 1024, 1024
E_QK, E_V = 512, 256
E_ALL = 2 * E_QK + E_V
GROUPS = 16
GROUP_CHANNELS = CHANNELS // GROUPS
EPS_GN = 1e-5
EPS_L2 = 1e-12

P = 128
PACK = 4
K_PASS = P * PACK
PASSES = CHANNELS // K_PASS
BLOCKS = CHANNELS // P
T = SEQ // P
TILES = BATCH * T
UNIT = 4
UNIT_COLS = UNIT * P
NORM_STEPS = 2 * PASSES
HALF_GROUP_COUNT = T * GROUP_CHANNELS // 2
W_ROW_TILES = E_ALL // P

LAG_WEIGHTS = 5
LAG_COEF = T
COEF_STEPS = 5
LAG_NORM = LAG_COEF + COEF_STEPS + 1
LAG_PROJECT = LAG_NORM + UNIT
LAG_FINISH = LAG_PROJECT + 1
SLOTS = TILES + LAG_FINISH

FLOPS = 2 * BATCH * SEQ * CHANNELS * E_ALL


def tile_retnetblock_pa_t_kernel(tc, x, gn1_g, gn1_b, wq, wk, wv, out_0, out_1, out_2):
    nc = tc.nc
    with ExitStack() as pools:
        pools.enter_context(tc.manual_schedule())
        const = pools.enter_context(tc.tile_pool(name="const", bufs=1))
        x_pool = pools.enter_context(tc.tile_pool(name="x", bufs=BATCH))
        w_pool = pools.enter_context(tc.tile_pool(name="w", bufs=3))
        stat = pools.enter_context(tc.tile_pool(name="stat", bufs=2))
        plane_pool = pools.enter_context(tc.tile_pool(name="planes", bufs=2))
        grouped_pool = pools.enter_context(tc.tile_pool(name="grouped", bufs=2))
        code_pool = pools.enter_context(tc.tile_pool(name="codes", bufs=3))
        norm_pool = pools.enter_context(tc.tile_pool(name="norm", bufs=4))
        out_pool = pools.enter_context(tc.tile_pool(name="out", bufs=4))
        turned_psum = pools.enter_context(tc.psum_pool(name="turned_psum", bufs=2))
        acc_psum = pools.enter_context(tc.psum_pool(name="acc_psum", bufs=5))
        v_psum = pools.enter_context(tc.psum_pool(name="v_psum", bufs=1))

        ident = const.tile([P, P], BF16)
        make_identity(nc, ident[:])
        ones = const.tile([P, P], F32)
        nc.vector.memset(ones[:], 1.0)
        half_ones = const.tile([P, 2, P], F32)
        nc.vector.memset(half_ones[:], 0.0)
        for h in range(2):
            nc.vector.memset(half_ones[:, h, h * (P // 2) : (h + 1) * (P // 2)], 1.0)
        minus_half = const.tile([P, BLOCKS], F32)
        nc.gpsimd.memset(minus_half[:], -0.5)

        w_codes = const.tile([P, PASSES, E_ALL], U32, align_bytes=64)
        w_scales = const.tile([P, PASSES, E_ALL], U8, align_bytes=64)

        x_sb = []
        for b in range(BATCH):
            x_b = x_pool.tile([P, T, CHANNELS], BF16)
            x_sb.append(x_b)

        def load_x(b):
            for cols in (slice(0, CHANNELS // 2), slice(CHANNELS // 2, CHANNELS)):
                nc.sync.dma_start(out=x_sb[b][:, :, cols], in_=x[b].rearrange("(m t) d -> m t d", t=T)[:, :, cols])

        load_x(0)
        gb_rows = const.tile([P, P], BF16)
        nc.vector.memset(gb_rows[:], 0.0)
        nc.sync.dma_start(out=gb_rows[0:BLOCKS, :], in_=gn1_g.rearrange("(c p) -> c p", p=P))
        nc.sync.dma_start(out=gb_rows[BLOCKS : 2 * BLOCKS, :], in_=gn1_b.rearrange("(c p) -> c p", p=P))
        w_row_tiles = []
        for w in (wq, wk, wv):
            n_tiles = w.shape[0] // P
            w_rows = const.tile([P, n_tiles, CHANNELS], BF16, name="w_rows_%d" % len(w_row_tiles))
            nc.sync.dma_start(out=w_rows[:], in_=w.rearrange("(r p) k -> p r k", p=P))
            col0 = len(w_row_tiles) * P
            for r in range(n_tiles):
                w_row_tiles.append((w_rows, r, n_tiles, col0))
        for b in range(1, BATCH):
            load_x(b)

        gb_t = turned_psum.tile([P, P], BF16, tag="turned")
        nc.tensor.transpose(gb_t[:], gb_rows[:], ident[:])
        gb = const.tile([P, 2 * BLOCKS], F32)
        nc.scalar.copy(out=gb[:], in_=gb_t[:, 0 : 2 * BLOCKS])

        st_of, coef_of, planes_of, grouped_of, codes_of, acc_of, v_of, out_of, w_grouped_of = {}, {}, {}, {}, {}, {}, {}, {}, {}

        def statistics_step(b, step):
            if step == 0:
                st_of[b] = stat.tile([P, GROUPS, 6], F32, name="st", bufs=BATCH)
            for g in range(step * GROUPS // T, (step + 1) * GROUPS // T):
                cols = slice(g * GROUP_CHANNELS, (g + 1) * GROUP_CHANNELS)
                nc.vector.bn_stats(out=st_of[b][:, g, :], in_=x_sb[b][:, :, cols])

        def weights_step(w_rows, r, n_tiles, col0):
            w_t = turned_psum.tile([P, BLOCKS, P], BF16, tag="turned")
            for c in range(BLOCKS):
                nc.tensor.transpose(w_t[:, c, :], w_rows[:, r, c * P : (c + 1) * P], ident[:])
            if r == 0:
                w_grouped_of[col0] = w_pool.tile([P, PASSES, n_tiles * P, PACK], BF16, name="w_grouped", align_bytes=64)
            w_grouped = w_grouped_of[col0]
            nc.scalar.copy(
                out=w_grouped[:, :, r * P : (r + 1) * P, :], in_=w_t[:].rearrange("p (g j) n -> p g n j", j=PACK)
            )
            if r == n_tiles - 1:
                cols = slice(col0, col0 + n_tiles * P)
                for g in range(PASSES):
                    nc.vector.quantize_mx(
                        out=w_codes[:, g, cols].bitcast(FP8X4),
                        scales=w_scales[:, g, cols],
                        in_=w_grouped[:, g, :, :].rearrange("p n j -> p (n j)"),
                    )

        def coefficients_step(b, step):
            halves = st_of[b][:].rearrange("p g (h s) -> p g h s", s=3)
            means = halves[:, :, :, 1]
            spreads = halves[:, :, :, 2]
            if step == 0:
                moments = stat.tile([P, 2, GROUPS], F32)
                nc.gpsimd.tensor_tensor(out=moments[:, 1, :], in0=means[:, :, 0], in1=means[:, :, 1], op=ALU.add)
                spread_sum = stat.tile([P, GROUPS], F32)
                nc.gpsimd.tensor_tensor(out=spread_sum[:], in0=spreads[:, :, 0], in1=spreads[:, :, 1], op=ALU.add)
                spread_part = stat.tile([P, GROUPS], F32)
                nc.gpsimd.tensor_scalar(
                    out=spread_part[:], in0=spread_sum[:], scalar1=1.0 / HALF_GROUP_COUNT, scalar2=0.0,
                    op0=ALU.mult, op1=ALU.add,
                )
                coef_of[b] = {"moments": moments, "spread_part": spread_part}
            elif step == 1:
                mean_sum = acc_psum.tile([P, GROUPS], F32, tag="acc")
                nc.tensor.matmul(out=mean_sum[:], lhsT=ones[:], rhs=coef_of[b]["moments"][:, 1, :], start=True, stop=True)
                coef_of[b]["mean_sum"] = mean_sum
            elif step == 2:
                moments = coef_of[b]["moments"]
                mean_all = stat.tile([P, GROUPS], F32)
                nc.scalar.activation(out=mean_all[:], in_=coef_of[b]["mean_sum"][:], func=ACT.Copy, scale=1.0 / (2 * P))
                dev = stat.tile([P, GROUPS, 2], F32)
                nc.gpsimd.tensor_tensor(
                    out=dev[:], in0=means, in1=mean_all[:].unsqueeze(2).to_broadcast([P, GROUPS, 2]), op=ALU.subtract
                )
                dev_sq = stat.tile([P, GROUPS, 2], F32)
                nc.gpsimd.tensor_tensor(out=dev_sq[:], in0=dev[:], in1=dev[:], op=ALU.mult)
                dev_sq_sum = stat.tile([P, GROUPS], F32)
                nc.gpsimd.tensor_tensor(out=dev_sq_sum[:], in0=dev_sq[:, :, 0], in1=dev_sq[:, :, 1], op=ALU.add)
                nc.gpsimd.tensor_tensor(
                    out=moments[:, 0, :], in0=dev_sq_sum[:], in1=coef_of[b]["spread_part"][:], op=ALU.add
                )
            elif step == 3:
                by_half = coef_of[b]["moments"][:].rearrange("p s (c h) -> p s c h", h=2)
                sums = acc_psum.tile([P, 2, BLOCKS], F32, tag="acc")
                for h in range(2):
                    nc.tensor.matmul(
                        out=sums[:], lhsT=half_ones[:, h, :], rhs=by_half[:, :, :, h], start=(h == 0), stop=(h == 1)
                    )
                coef_of[b]["sums"] = sums
            else:
                sums = coef_of[b]["sums"]
                var_eps = stat.tile([P, BLOCKS], F32)
                nc.scalar.activation(out=var_eps[:], in_=sums[:, 0, :], func=ACT.Copy, scale=1.0 / (2 * P), bias=EPS_GN)
                mean = stat.tile([P, BLOCKS], F32)
                nc.scalar.activation(out=mean[:], in_=sums[:, 1, :], func=ACT.Copy, scale=1.0 / (2 * P))
                rstd = stat.tile([P, BLOCKS], F32)
                nc.gpsimd.tensor_tensor(out=rstd[:], in0=var_eps[:], in1=minus_half[:], op=ALU.pow)
                gain = stat.tile([P, BLOCKS], F32)
                nc.gpsimd.tensor_tensor(out=gain[:], in0=gb[:, 0:BLOCKS], in1=rstd[:], op=ALU.mult)
                mean_gain = stat.tile([P, BLOCKS], F32)
                nc.gpsimd.tensor_tensor(out=mean_gain[:], in0=mean[:], in1=gain[:], op=ALU.mult)
                shift = stat.tile([P, BLOCKS], F32)
                nc.gpsimd.tensor_tensor(out=shift[:], in0=gb[:, BLOCKS : 2 * BLOCKS], in1=mean_gain[:], op=ALU.subtract)
                coef_of[b]["gain"] = gain
                coef_of[b]["shift"] = shift

        def normalise_step(u, step, by_scalar):
            b, t0 = u // (T // UNIT), (u % (T // UNIT)) * UNIT
            g = step // 2
            if step % 2 == 0:
                banks = []
                for half in range(2):
                    x_t = turned_psum.tile([P, PACK // 2, UNIT, P], BF16, tag="turned")
                    banks.append(x_t)
                for j in range(PACK):
                    c = g * PACK + j
                    for t in range(UNIT):
                        nc.tensor.transpose(
                            banks[j // 2][:, j % 2, t, :], x_sb[b][:, t0 + t, c * P : (c + 1) * P], ident[:]
                        )
                planes_of[u] = plane_pool.tile([P, PACK, UNIT_COLS], BF16, name="planes")
                for j in range(PACK):
                    c = g * PACK + j
                    h_plane = planes_of[u][:, j, :]
                    x_plane = banks[j // 2][:, j % 2, :, :].rearrange("p t m -> p (t m)")
                    gain = coef_of[b]["gain"][:, c : c + 1]
                    shift = coef_of[b]["shift"][:, c : c + 1]
                    if by_scalar:
                        nc.scalar.activation(out=h_plane, in_=x_plane, func=ACT.Identity, scale=gain, bias=shift)
                    else:
                        nc.vector.tensor_scalar(
                            out=h_plane, in0=x_plane, scalar1=gain, scalar2=shift, op0=ALU.mult, op1=ALU.add
                        )
            else:
                grouped_of[u] = grouped_pool.tile([P, UNIT_COLS, PACK], BF16, name="grouped", align_bytes=64)
                nc.vector.tensor_copy(
                    out=grouped_of[u][:].rearrange("p (c i) j -> p c j i", i=4),
                    in_=planes_of[u][:].rearrange("p j (c i) -> p c j i", i=4),
                )

        def quantise_step(u, step):
            if step % 2 == 0:
                return
            g = step // 2
            if g == 0:
                h_codes = code_pool.tile([P, PASSES, UNIT_COLS], U32, align_bytes=64)
                h_scales = code_pool.tile([P, PASSES, UNIT_COLS], U8, align_bytes=64)
                codes_of[u] = (h_codes, h_scales)
            h_codes, h_scales = codes_of[u]
            nc.vector.quantize_mx(
                out=h_codes[:, g, :].bitcast(FP8X4),
                scales=h_scales[:, g, :],
                in_=grouped_of[u][:].rearrange("p c j -> p (c j)"),
            )

        def project(acc, tile, cols):
            h_codes, h_scales = codes_of[tile // UNIT]
            rows = slice((tile % UNIT) * P, (tile % UNIT + 1) * P)
            for g in range(PASSES):
                nc.tensor.matmul_mx(
                    out=acc,
                    lhsT=h_codes[:, g, rows].bitcast(FP8X4),
                    lhsT_scale=h_scales[:, g, rows],
                    rhs=w_codes[:, g, cols].bitcast(FP8X4),
                    rhs_scale=w_scales[:, g, cols],
                    start=(g == 0),
                    stop=(g == PASSES - 1),
                )

        def project_step(tile):
            q_acc = acc_psum.tile([P, E_QK], F32, tag="acc")
            k_acc = acc_psum.tile([P, E_QK], F32, tag="acc")
            if tile % 2 == 0:
                v_of[tile // 2] = v_psum.tile([P, 2, E_V], F32, name="v_acc")
            project(q_acc[:], tile, slice(0, E_QK))
            project(k_acc[:], tile, slice(E_QK, 2 * E_QK))
            project(v_of[tile // 2][:, tile % 2, :], tile, slice(2 * E_QK, E_ALL))
            sum_sq = norm_pool.tile([P, 2], F32)
            for col, acc in enumerate((q_acc, k_acc)):
                squares = norm_pool.tile([P, E_QK], BF16)
                nc.scalar.activation(out=squares[:], in_=acc[:], func=ACT.Square, accum_out=sum_sq[:, col : col + 1])
            floored = norm_pool.tile([P, 2], F32)
            nc.gpsimd.tensor_scalar_max(out=floored[:], in0=sum_sq[:], scalar1=EPS_L2 * EPS_L2)
            inv_norm = norm_pool.tile([P, 2], F32)
            nc.gpsimd.tensor_tensor(out=inv_norm[:], in0=floored[:], in1=minus_half[:, 0:2], op=ALU.pow)
            acc_of[tile] = (q_acc, k_acc, inv_norm)

        def store(dram, tile, tile_out):
            b, t = tile // T, tile % T
            nc.sync.dma_start(out=dram[b].rearrange("(m t) e -> m t e", t=T)[:, t - 1 : t + 1, :], in_=tile_out[:])

        def copy_v_step(tile):
            if tile % 2 == 1:
                v_out = out_of[tile // 2][2]
                nc.scalar.copy(out=v_out[:], in_=v_of[tile // 2][:])
                store(out_2, tile, v_out)

        def finish_step(tile, k_by_vector):
            if tile % 2 == 0:
                q_out = out_pool.tile([P, 2, E_QK], F32)
                k_out = out_pool.tile([P, 2, E_QK], F32)
                v_out = out_pool.tile([P, 2, E_V], F32)
                out_of[tile // 2] = (q_out, k_out, v_out)
            q_out, k_out, v_out = out_of[tile // 2]
            q_acc, k_acc, inv_norm = acc_of[tile]
            nc.scalar.activation(out=q_out[:, tile % 2, :], in_=q_acc[:], func=ACT.Copy, scale=inv_norm[:, 0:1])
            if k_by_vector:
                nc.vector.tensor_scalar_mul(out=k_out[:, tile % 2, :], in0=k_acc[:], scalar1=inv_norm[:, 1:2])
            else:
                nc.scalar.activation(out=k_out[:, tile % 2, :], in_=k_acc[:], func=ACT.Copy, scale=inv_norm[:, 1:2])
            if tile % 2 == 1:
                store(out_0, tile, q_out)
                store(out_1, tile, k_out)

        for n in range(SLOTS):
            if n >= LAG_FINISH:
                copy_v_step(n - LAG_FINISH)
            if 0 <= n - LAG_NORM < TILES:
                normalise_step((n - LAG_NORM) // NORM_STEPS, (n - LAG_NORM) % NORM_STEPS, n < LAG_PROJECT)
            if 0 <= n - LAG_COEF < TILES and (n - LAG_COEF) % T < COEF_STEPS:
                coefficients_step((n - LAG_COEF) // T, (n - LAG_COEF) % T)
            if n < TILES:
                statistics_step(n // T, n % T)
            if 0 <= n - LAG_WEIGHTS < W_ROW_TILES:
                weights_step(*w_row_tiles[n - LAG_WEIGHTS])
            if 0 <= n - LAG_NORM < TILES:
                quantise_step((n - LAG_NORM) // NORM_STEPS, (n - LAG_NORM) % NORM_STEPS)
            if 0 <= n - LAG_PROJECT < TILES:
                project_step(n - LAG_PROJECT)
            if n >= LAG_FINISH:
                finish_step(n - LAG_FINISH, n >= TILES)
